import numpy as np
import ml_dtypes


def mxq(x, axis, fmt="e4m3"):
    dtype, down = {"e4m3": (ml_dtypes.float8_e4m3fn, 7), "e5m2": (ml_dtypes.float8_e5m2, 14)}[fmt]
    v = np.moveaxis(np.asarray(x, np.float32).astype(ml_dtypes.bfloat16).astype(np.float64), axis, -1)
    blocks = v.reshape(v.shape[:-1] + (-1, 32))
    amax = np.abs(blocks).max(-1, keepdims=True)
    byte = np.maximum(np.where(amax > 0, np.frexp(amax)[1] - 1 + 127, 0) - down, 1)
    scale = np.exp2(byte - 127.0)
    codes = (blocks / scale).astype(np.float32).astype(dtype).astype(np.float64)
    return np.moveaxis((codes * scale).reshape(v.shape), -1, axis)


WIDE = False


def mx_kscale(k):
    if not WIDE:
        return np.ones(k)
    levels = np.array([10, -10, 5, -5, 0])
    a = np.random.permutation(np.resize(levels, k // 512 * 4)).reshape(k // 512, 4)
    idx = np.arange(k)
    return np.exp2(a[idx // 512, idx % 128 // 32])


BF16 = ml_dtypes.bfloat16


def bf(x):
    return np.asarray(x, np.float32).astype(BF16)


def f64(x):
    return np.asarray(x).astype(np.float64)


B, T, D, M, C = 2, 128, 512, 512, 8192


def sigmoid(v):
    return 1.0 / (1.0 + np.exp(-v))


def setup_inputs():
    t = mx_kscale(M)
    go_w = np.concatenate([np.random.standard_normal((M, D)) / np.sqrt(D),
                           np.random.standard_normal((M, M)) * 2.0 / np.sqrt(M) / t], axis=1)
    return {"h": bf(np.random.standard_normal((B, T, D))),
            "gated_mem": bf(np.random.standard_normal((B, T, M)) * 0.4 * t),
            "go_w": bf(go_w),
            "go_b": bf(np.random.standard_normal(M) * 0.5),
            "out_w": bf(np.random.standard_normal((D, M)) * 5.0 / np.sqrt(M) / t),
            "out_b": bf(np.random.standard_normal(D) * 0.5)}


def reference(h, gated_mem, go_w, go_b, out_w, out_b):
    h = f64(h)
    g = f64(gated_mem)
    gate_in = np.concatenate([h, g], axis=-1)
    gate_w = sigmoid((mxq(gate_in, 2, "e4m3") @ mxq(f64(go_w), 1, "e4m3").T) + f64(go_b))
    return h + (mxq(gate_w * g, 2, "e4m3") @ mxq(f64(out_w), 1, "e4m3").T) + f64(out_b)

@@ -1,0 +1,163 @@
+from contextlib import ExitStack
+
+import concourse.masks as masks
+import concourse.mybir as mybir
+
+F32 = mybir.dt.float32
+BF16 = mybir.dt.bfloat16
+U32 = mybir.dt.uint32
+U8 = mybir.dt.uint8
+FP8X4 = mybir.dt.float8_e4m3fn_x4
+
+P = 128
+PACK = 4
+TOKENS = 256
+D = 512
+M = 512
+TOKEN_TILES = TOKENS // P
+GATE_TILES = M // P
+UNIT = 1024
+BLOCKS = 4
+
+FLOPS = 2 * TOKENS * (D + M) * M + 2 * TOKENS * M * D
+
+
+def transpose_and_quantise(nc, psum, ident, copy, rows, grouped, codes, scales):
+    words = rows.bitcast(F32)
+    bank = psum.tile([P, BLOCKS, P], F32, tag="bank")
+    for b in range(BLOCKS):
+        nc.tensor.transpose(bank[:, b, :], words[:, b * P : (b + 1) * P], ident)
+    copy(
+        out=grouped.bitcast(F32).rearrange("q (a c u) -> q a c u", a=2, u=2),
+        in_=bank[:].rearrange("q (a u) c -> q a c u", u=2),
+    )
+    nc.vector.quantize_mx(out=codes.bitcast(FP8X4), scales=scales, in_=grouped)
+
+
+def tile_aurelianmemorycore_pb_s_kernel(tc, h, gated_mem, go_w, go_b, out_w, out_b, out):
+    nc = tc.nc
+    with ExitStack() as ctx:
+        keep = ctx.enter_context(tc.tile_pool(name="keep", bufs=1))
+        psum = ctx.enter_context(tc.psum_pool(name="psum", bufs=8))
+
+        h_rows = keep.tile([P, UNIT], BF16)
+        g_rows = keep.tile([P, UNIT], BF16)
+        nc.sync.dma_start(out=h_rows[:], in_=h.flatten_outer_dims().rearrange("(p j) d -> p (j d)", j=TOKEN_TILES))
+        nc.sync.dma_start(
+            out=g_rows[:], in_=gated_mem.flatten_outer_dims().rearrange("(p j) d -> p (j d)", j=TOKEN_TILES)
+        )
+        go_w_tiles = go_w.rearrange("(u p e) k -> u e p k", u=2, e=2)
+        w_rows = []
+        for t in range(GATE_TILES):
+            rows = keep.tile([P, UNIT], BF16, name="w_rows%d" % t)
+            nc.sync.dma_start(out=rows[:], in_=go_w_tiles[t // 2, t % 2])
+            w_rows.append(rows)
+        out_w_tiles = out_w.rearrange("(r p) m -> p r m", p=P)
+        o_rows = []
+        for half in range(2):
+            rows = keep.tile([P, UNIT], BF16, name="o_rows%d" % half)
+            nc.sync.dma_start(
+                out=rows[:].rearrange("p (r m) -> p r m", r=2), in_=out_w_tiles[:, 2 * half : 2 * half + 2, :]
+            )
+            o_rows.append(rows)
+
+        out_b_row = keep.tile([P, D], BF16)
+        nc.vector.memset(out_b_row[:], 0.0)
+        nc.scalar.dma_start(out=out_b_row[0:1, :], in_=out_b.rearrange("(o d) -> o d", o=1))
+        ones = keep.tile([P, P], BF16)
+        nc.vector.memset(ones[:], 1.0)
+        go_b_bf = keep.tile([P, GATE_TILES], BF16)
+        nc.scalar.dma_start(
+            out=go_b_bf[:].rearrange("p (u e) -> p u e", u=2), in_=go_b.rearrange("(u p e) -> p u e", u=2, e=2)
+        )
+        go_b_f32 = keep.tile([P, GATE_TILES], F32)
+        nc.vector.tensor_copy(out=go_b_f32[:], in_=go_b_bf[:])
+
+        ident = keep.tile([P, P], F32)
+        masks.make_identity(nc, ident[:])
+
+        warm = keep.tile([P, 1], F32)
+        nc.vector.memset(warm[:], 0.0)
+        nc.scalar.activation(out=warm[:], in_=warm[:], func=mybir.ActivationFunctionType.Sigmoid)
+
+        out_b_bank = psum.tile([P, D], F32, tag="bank")
+        nc.tensor.matmul(out=out_b_bank[:], lhsT=ones[:], rhs=out_b_row[:], start=True, stop=True)
+        residual = keep.tile([P, TOKEN_TILES, D], F32)
+        for j in range(TOKEN_TILES):
+            nc.vector.tensor_tensor(
+                out=residual[:, j, :], in0=h_rows[:, j * D : (j + 1) * D], in1=out_b_bank[:], op=mybir.AluOpType.add
+            )
+
+        x_grouped = []
+        x_codes = []
+        x_scales = []
+        for c, rows in enumerate((h_rows, g_rows)):
+            grouped = keep.tile([P, UNIT], BF16, name="x_grouped%d" % c, align_bytes=64)
+            codes = keep.tile([P, TOKENS], U32, name="x_codes%d" % c, align_bytes=64)
+            scales = keep.tile([P, TOKENS], U8, name="x_scales%d" % c, align_bytes=64)
+            transpose_and_quantise(nc, psum, ident[:], nc.scalar.copy, rows[:], grouped[:], codes[:], scales[:])
+            x_grouped.append(grouped)
+            x_codes.append(codes)
+            x_scales.append(scales)
+        g_grouped = x_grouped[1]
+
+        gate = keep.tile([P, GATE_TILES, TOKENS], F32)
+        for t in range(GATE_TILES):
+            grouped = keep.tile([P, UNIT], BF16, name="w_grouped%d" % t, align_bytes=64)
+            codes = keep.tile([P, 2 * P], U32, name="w_codes%d" % t, align_bytes=64)
+            scales = keep.tile([P, 2 * P], U8, name="w_scales%d" % t, align_bytes=64)
+            transpose_and_quantise(nc, psum, ident[:], nc.scalar.copy, w_rows[t][:], grouped[:], codes[:], scales[:])
+            acc = psum.tile([P, TOKENS], F32, tag="bank")
+            for c in range(2):
+                nc.tensor.matmul_mx(
+                    out=acc[:],
+                    lhsT=codes[:, c * P : (c + 1) * P].bitcast(FP8X4),
+                    lhsT_scale=scales[:, c * P : (c + 1) * P],
+                    rhs=x_codes[c][:].bitcast(FP8X4),
+                    rhs_scale=x_scales[c][:],
+                    start=(c == 0),
+                    stop=(c == 1),
+                )
+            nc.scalar.activation(
+                out=gate[:, t, :],
+                in_=acc[:],
+                func=mybir.ActivationFunctionType.Sigmoid,
+                bias=go_b_f32[:, t : t + 1],
+                scale=1.0,
+            )
+
+        o_codes = keep.tile([P, D], U32, align_bytes=64)
+        o_scales = keep.tile([P, D], U8, align_bytes=64)
+        for half in range(2):
+            grouped = keep.tile([P, UNIT], BF16, name="o_grouped%d" % half, align_bytes=64)
+            cols = slice(half * 2 * P, (half + 1) * 2 * P)
+            transpose_and_quantise(
+                nc, psum, ident[:], nc.vector.tensor_copy, o_rows[half][:], grouped[:], o_codes[:, cols], o_scales[:, cols]
+            )
+
+        out_rows = out.flatten_outer_dims().rearrange("(p j) d -> p j d", j=TOKEN_TILES)
+        for j in range(TOKEN_TILES):
+            cols = slice(j * P, (j + 1) * P)
+            gated = keep.tile([P, P * PACK], BF16, name="gated%d" % j, align_bytes=64)
+            nc.vector.tensor_tensor(
+                out=gated[:].rearrange("q (c t) -> q c t", t=PACK),
+                in0=gate[:, :, cols].rearrange("q t c -> q c t"),
+                in1=g_grouped[:, j * P * PACK : (j + 1) * P * PACK].rearrange("q (c t) -> q c t", t=PACK),
+                op=mybir.AluOpType.mult,
+            )
+            codes = keep.tile([P, P], U32, name="gated_codes%d" % j, align_bytes=64)
+            scales = keep.tile([P, P], U8, name="gated_scales%d" % j, align_bytes=64)
+            nc.vector.quantize_mx(out=codes[:].bitcast(FP8X4), scales=scales[:], in_=gated[:])
+            acc = psum.tile([P, D], F32, tag="bank")
+            nc.tensor.matmul_mx(
+                out=acc[:],
+                lhsT=codes[:].bitcast(FP8X4),
+                lhsT_scale=scales[:],
+                rhs=o_codes[:].bitcast(FP8X4),
+                rhs_scale=o_scales[:],
+                start=True,
+                stop=True,
+            )
+            result = keep.tile([P, D], F32, name="result%d" % j)
+            nc.vector.tensor_tensor(out=result[:], in0=acc[:], in1=residual[:, j, :], op=mybir.AluOpType.add)
+            nc.sync.dma_start(out=out_rows[:, j, :], in_=result[:])

@@ -22,12 +22,12 @@ BLOCKS = 4
 FLOPS = 2 * TOKENS * (D + M) * M + 2 * TOKENS * M * D
 
 
-def transpose_and_quantise(nc, psum, ident, copy, rows, grouped, codes, scales):
+def transpose_and_quantise(nc, psum, ident, rows, grouped, codes, scales):
     words = rows.bitcast(F32)
     bank = psum.tile([P, BLOCKS, P], F32, tag="bank")
     for b in range(BLOCKS):
         nc.tensor.transpose(bank[:, b, :], words[:, b * P : (b + 1) * P], ident)
-    copy(
+    nc.scalar.copy(
         out=grouped.bitcast(F32).rearrange("q (a c u) -> q a c u", a=2, u=2),
         in_=bank[:].rearrange("q (a u) c -> q a c u", u=2),
     )
@@ -39,6 +39,15 @@ def tile_aurelianmemorycore_pb_s_kernel(tc, h, gated_mem, go_w, go_b, out_w, out
     with ExitStack() as ctx:
         keep = ctx.enter_context(tc.tile_pool(name="keep", bufs=1))
         psum = ctx.enter_context(tc.psum_pool(name="psum", bufs=8))
+        ctx.enter_context(tc.manual_schedule())
+
+        out_b_row = keep.tile([P, D], BF16)
+        nc.vector.memset(out_b_row[:], 0.0)
+        nc.scalar.dma_start(out=out_b_row[0:1, :], in_=out_b.rearrange("(o d) -> o d", o=1))
+        go_b_bf = keep.tile([P, GATE_TILES], BF16)
+        nc.scalar.dma_start(
+            out=go_b_bf[:].rearrange("p (u e) -> p u e", u=2), in_=go_b.rearrange("(u p e) -> p u e", u=2, e=2)
+        )
 
         h_rows = keep.tile([P, UNIT], BF16)
         g_rows = keep.tile([P, UNIT], BF16)
@@ -61,21 +70,10 @@ def tile_aurelianmemorycore_pb_s_kernel(tc, h, gated_mem, go_w, go_b, out_w, out
             )
             o_rows.append(rows)
 
-        out_b_row = keep.tile([P, D], BF16)
-        nc.vector.memset(out_b_row[:], 0.0)
-        nc.scalar.dma_start(out=out_b_row[0:1, :], in_=out_b.rearrange("(o d) -> o d", o=1))
         ones = keep.tile([P, P], BF16)
         nc.vector.memset(ones[:], 1.0)
-        go_b_bf = keep.tile([P, GATE_TILES], BF16)
-        nc.scalar.dma_start(
-            out=go_b_bf[:].rearrange("p (u e) -> p u e", u=2), in_=go_b.rearrange("(u p e) -> p u e", u=2, e=2)
-        )
-        go_b_f32 = keep.tile([P, GATE_TILES], F32)
-        nc.vector.tensor_copy(out=go_b_f32[:], in_=go_b_bf[:])
-
         ident = keep.tile([P, P], F32)
         masks.make_identity(nc, ident[:])
-
         warm = keep.tile([P, 1], F32)
         nc.vector.memset(warm[:], 0.0)
         nc.scalar.activation(out=warm[:], in_=warm[:], func=mybir.ActivationFunctionType.Sigmoid)
@@ -95,24 +93,40 @@ def tile_aurelianmemorycore_pb_s_kernel(tc, h, gated_mem, go_w, go_b, out_w, out
             grouped = keep.tile([P, UNIT], BF16, name="x_grouped%d" % c, align_bytes=64)
             codes = keep.tile([P, TOKENS], U32, name="x_codes%d" % c, align_bytes=64)
             scales = keep.tile([P, TOKENS], U8, name="x_scales%d" % c, align_bytes=64)
-            transpose_and_quantise(nc, psum, ident[:], nc.scalar.copy, rows[:], grouped[:], codes[:], scales[:])
+            transpose_and_quantise(nc, psum, ident[:], rows[:], grouped[:], codes[:], scales[:])
             x_grouped.append(grouped)
             x_codes.append(codes)
             x_scales.append(scales)
         g_grouped = x_grouped[1]
 
-        gate = keep.tile([P, GATE_TILES, TOKENS], F32)
+        go_b_f32 = keep.tile([P, GATE_TILES], F32)
+        nc.vector.tensor_copy(out=go_b_f32[:], in_=go_b_bf[:])
+
+        w_codes = []
+        w_scales = []
         for t in range(GATE_TILES):
             grouped = keep.tile([P, UNIT], BF16, name="w_grouped%d" % t, align_bytes=64)
             codes = keep.tile([P, 2 * P], U32, name="w_codes%d" % t, align_bytes=64)
             scales = keep.tile([P, 2 * P], U8, name="w_scales%d" % t, align_bytes=64)
-            transpose_and_quantise(nc, psum, ident[:], nc.scalar.copy, w_rows[t][:], grouped[:], codes[:], scales[:])
+            transpose_and_quantise(nc, psum, ident[:], w_rows[t][:], grouped[:], codes[:], scales[:])
+            w_codes.append(codes)
+            w_scales.append(scales)
+
+        o_codes = keep.tile([P, D], U32, align_bytes=64)
+        o_scales = keep.tile([P, D], U8, align_bytes=64)
+        for half in range(2):
+            grouped = keep.tile([P, UNIT], BF16, name="o_grouped%d" % half, align_bytes=64)
+            cols = slice(half * 2 * P, (half + 1) * 2 * P)
+            transpose_and_quantise(nc, psum, ident[:], o_rows[half][:], grouped[:], o_codes[:, cols], o_scales[:, cols])
+
+        gate = keep.tile([P, GATE_TILES, TOKENS], F32)
+        for t in range(GATE_TILES):
             acc = psum.tile([P, TOKENS], F32, tag="bank")
             for c in range(2):
                 nc.tensor.matmul_mx(
                     out=acc[:],
-                    lhsT=codes[:, c * P : (c + 1) * P].bitcast(FP8X4),
-                    lhsT_scale=scales[:, c * P : (c + 1) * P],
+                    lhsT=w_codes[t][:, c * P : (c + 1) * P].bitcast(FP8X4),
+                    lhsT_scale=w_scales[t][:, c * P : (c + 1) * P],
                     rhs=x_codes[c][:].bitcast(FP8X4),
                     rhs_scale=x_scales[c][:],
                     start=(c == 0),
@@ -126,16 +140,7 @@ def tile_aurelianmemorycore_pb_s_kernel(tc, h, gated_mem, go_w, go_b, out_w, out
                 scale=1.0,
             )
 
-        o_codes = keep.tile([P, D], U32, align_bytes=64)
-        o_scales = keep.tile([P, D], U8, align_bytes=64)
-        for half in range(2):
-            grouped = keep.tile([P, UNIT], BF16, name="o_grouped%d" % half, align_bytes=64)
-            cols = slice(half * 2 * P, (half + 1) * 2 * P)
-            transpose_and_quantise(
-                nc, psum, ident[:], nc.vector.tensor_copy, o_rows[half][:], grouped[:], o_codes[:, cols], o_scales[:, cols]
-            )
-
-        out_rows = out.flatten_outer_dims().rearrange("(p j) d -> p j d", j=TOKEN_TILES)
+        out_acc = []
         for j in range(TOKEN_TILES):
             cols = slice(j * P, (j + 1) * P)
             gated = keep.tile([P, P * PACK], BF16, name="gated%d" % j, align_bytes=64)
@@ -158,6 +163,10 @@ def tile_aurelianmemorycore_pb_s_kernel(tc, h, gated_mem, go_w, go_b, out_w, out
                 start=True,
                 stop=True,
             )
+            out_acc.append(acc)
+
+        out_rows = out.flatten_outer_dims().rearrange("(p j) d -> p j d", j=TOKEN_TILES)
+        for j in range(TOKEN_TILES):
             result = keep.tile([P, D], F32, name="result%d" % j)
-            nc.vector.tensor_tensor(out=result[:], in0=acc[:], in1=residual[:, j, :], op=mybir.AluOpType.add)
+            nc.vector.tensor_tensor(out=result[:], in0=out_acc[j][:], in1=residual[:, j, :], op=mybir.AluOpType.add)
             nc.sync.dma_start(out=out_rows[:, j, :], in_=result[:])

@@ -22,12 +22,12 @@ BLOCKS = 4
 FLOPS = 2 * TOKENS * (D + M) * M + 2 * TOKENS * M * D
 
 
-def transpose_and_quantise(nc, psum, ident, rows, grouped, codes, scales):
+def transpose_and_quantise(nc, psum, ident, copy, rows, grouped, codes, scales):
     words = rows.bitcast(F32)
     bank = psum.tile([P, BLOCKS, P], F32, tag="bank")
     for b in range(BLOCKS):
         nc.tensor.transpose(bank[:, b, :], words[:, b * P : (b + 1) * P], ident)
-    nc.scalar.copy(
+    copy(
         out=grouped.bitcast(F32).rearrange("q (a c u) -> q a c u", a=2, u=2),
         in_=bank[:].rearrange("q (a u) c -> q a c u", u=2),
     )
@@ -78,13 +78,6 @@ def tile_aurelianmemorycore_pb_s_kernel(tc, h, gated_mem, go_w, go_b, out_w, out
         nc.vector.memset(warm[:], 0.0)
         nc.scalar.activation(out=warm[:], in_=warm[:], func=mybir.ActivationFunctionType.Sigmoid)
 
-        out_b_bank = psum.tile([P, D], F32, tag="bank")
-        nc.tensor.matmul(out=out_b_bank[:], lhsT=ones[:], rhs=out_b_row[:], start=True, stop=True)
-        residual = keep.tile([P, TOKEN_TILES, D], F32)
-        for j in range(TOKEN_TILES):
-            nc.vector.tensor_tensor(
-                out=residual[:, j, :], in0=h_rows[:, j * D : (j + 1) * D], in1=out_b_bank[:], op=mybir.AluOpType.add
-            )
 
         x_grouped = []
         x_codes = []
@@ -93,11 +86,19 @@ def tile_aurelianmemorycore_pb_s_kernel(tc, h, gated_mem, go_w, go_b, out_w, out
             grouped = keep.tile([P, UNIT], BF16, name="x_grouped%d" % c, align_bytes=64)
             codes = keep.tile([P, TOKENS], U32, name="x_codes%d" % c, align_bytes=64)
             scales = keep.tile([P, TOKENS], U8, name="x_scales%d" % c, align_bytes=64)
-            transpose_and_quantise(nc, psum, ident[:], rows[:], grouped[:], codes[:], scales[:])
+            transpose_and_quantise(nc, psum, ident[:], nc.scalar.copy, rows[:], grouped[:], codes[:], scales[:])
             x_grouped.append(grouped)
             x_codes.append(codes)
             x_scales.append(scales)
         g_grouped = x_grouped[1]
+
+        out_b_bank = psum.tile([P, D], F32, tag="bank")
+        nc.tensor.matmul(out=out_b_bank[:], lhsT=ones[:], rhs=out_b_row[:], start=True, stop=True)
+        residual = keep.tile([P, TOKEN_TILES, D], F32)
+        for j in range(TOKEN_TILES):
+            nc.vector.tensor_tensor(
+                out=residual[:, j, :], in0=h_rows[:, j * D : (j + 1) * D], in1=out_b_bank[:], op=mybir.AluOpType.add
+            )
 
         go_b_f32 = keep.tile([P, GATE_TILES], F32)
         nc.vector.tensor_copy(out=go_b_f32[:], in_=go_b_bf[:])
@@ -108,7 +109,7 @@ def tile_aurelianmemorycore_pb_s_kernel(tc, h, gated_mem, go_w, go_b, out_w, out
             grouped = keep.tile([P, UNIT], BF16, name="w_grouped%d" % t, align_bytes=64)
             codes = keep.tile([P, 2 * P], U32, name="w_codes%d" % t, align_bytes=64)
             scales = keep.tile([P, 2 * P], U8, name="w_scales%d" % t, align_bytes=64)
-            transpose_and_quantise(nc, psum, ident[:], w_rows[t][:], grouped[:], codes[:], scales[:])
+            transpose_and_quantise(nc, psum, ident[:], nc.scalar.copy, w_rows[t][:], grouped[:], codes[:], scales[:])
             w_codes.append(codes)
             w_scales.append(scales)
 
@@ -117,7 +118,8 @@ def tile_aurelianmemorycore_pb_s_kernel(tc, h, gated_mem, go_w, go_b, out_w, out
         for half in range(2):
             grouped = keep.tile([P, UNIT], BF16, name="o_grouped%d" % half, align_bytes=64)
             cols = slice(half * 2 * P, (half + 1) * 2 * P)
-            transpose_and_quantise(nc, psum, ident[:], o_rows[half][:], grouped[:], o_codes[:, cols], o_scales[:, cols])
+            copy = nc.scalar.copy if half == 0 else nc.vector.tensor_copy
+            transpose_and_quantise(nc, psum, ident[:], copy, o_rows[half][:], grouped[:], o_codes[:, cols], o_scales[:, cols])
 
         gate = keep.tile([P, GATE_TILES, TOKENS], F32)
         for t in range(GATE_TILES):

@@ -6,6 +6,7 @@ import concourse.mybir as mybir
 F32 = mybir.dt.float32
 BF16 = mybir.dt.bfloat16
 U32 = mybir.dt.uint32
+I32 = mybir.dt.int32
 U8 = mybir.dt.uint8
 FP8X4 = mybir.dt.float8_e4m3fn_x4
 
@@ -41,17 +42,16 @@ def tile_aurelianmemorycore_pb_s_kernel(tc, h, gated_mem, go_w, go_b, out_w, out
         psum = ctx.enter_context(tc.psum_pool(name="psum", bufs=8))
         ctx.enter_context(tc.manual_schedule())
 
-        out_b_row = keep.tile([P, D], BF16)
-        nc.vector.memset(out_b_row[:], 0.0)
-        nc.scalar.dma_start(out=out_b_row[0:1, :], in_=out_b.rearrange("(o d) -> o d", o=1))
-        go_b_bf = keep.tile([P, GATE_TILES], BF16)
-        nc.scalar.dma_start(
-            out=go_b_bf[:].rearrange("p (u e) -> p u e", u=2), in_=go_b.rearrange("(u p e) -> p u e", u=2, e=2)
-        )
+        bias_rows = keep.tile([P, D + GATE_TILES * P // 2], BF16)
+        nc.vector.memset(bias_rows[:].bitcast(I32), 0)
+        out_b_row = bias_rows[:, 0:D]
+        go_b_rows = bias_rows[:, D : D + 2 * P]
+        nc.scalar.dma_start(out=go_b_rows[0:2, :], in_=go_b.rearrange("(u k) -> u k", u=2))
 
         h_rows = keep.tile([P, UNIT], BF16)
         g_rows = keep.tile([P, UNIT], BF16)
         nc.sync.dma_start(out=h_rows[:], in_=h.flatten_outer_dims().rearrange("(p j) d -> p (j d)", j=TOKEN_TILES))
+        nc.sync.dma_start(out=out_b_row[0:1, :], in_=out_b.rearrange("(o d) -> o d", o=1))
         nc.sync.dma_start(
             out=g_rows[:], in_=gated_mem.flatten_outer_dims().rearrange("(p j) d -> p (j d)", j=TOKEN_TILES)
         )
@@ -82,7 +82,15 @@ def tile_aurelianmemorycore_pb_s_kernel(tc, h, gated_mem, go_w, go_b, out_w, out
         x_grouped = []
         x_codes = []
         x_scales = []
+        residual = keep.tile([P, TOKEN_TILES, D], F32)
         for c, rows in enumerate((h_rows, g_rows)):
+            if c == 1:
+                out_b_bank = psum.tile([P, D], F32, tag="bank")
+                nc.tensor.matmul(out=out_b_bank[:], lhsT=ones[:], rhs=out_b_row, start=True, stop=True)
+                for j in range(TOKEN_TILES):
+                    nc.vector.tensor_tensor(
+                        out=residual[:, j, :], in0=h_rows[:, j * D : (j + 1) * D], in1=out_b_bank[:], op=mybir.AluOpType.add
+                    )
             grouped = keep.tile([P, UNIT], BF16, name="x_grouped%d" % c, align_bytes=64)
             codes = keep.tile([P, TOKENS], U32, name="x_codes%d" % c, align_bytes=64)
             scales = keep.tile([P, TOKENS], U8, name="x_scales%d" % c, align_bytes=64)
@@ -92,16 +100,10 @@ def tile_aurelianmemorycore_pb_s_kernel(tc, h, gated_mem, go_w, go_b, out_w, out
             x_scales.append(scales)
         g_grouped = x_grouped[1]
 
-        out_b_bank = psum.tile([P, D], F32, tag="bank")
-        nc.tensor.matmul(out=out_b_bank[:], lhsT=ones[:], rhs=out_b_row[:], start=True, stop=True)
-        residual = keep.tile([P, TOKEN_TILES, D], F32)
-        for j in range(TOKEN_TILES):
-            nc.vector.tensor_tensor(
-                out=residual[:, j, :], in0=h_rows[:, j * D : (j + 1) * D], in1=out_b_bank[:], op=mybir.AluOpType.add
-            )
-
-        go_b_f32 = keep.tile([P, GATE_TILES], F32)
-        nc.vector.tensor_copy(out=go_b_f32[:], in_=go_b_bf[:])
+        go_b_bank = psum.tile([P, P], F32, tag="bank")
+        nc.tensor.transpose(go_b_bank[:], go_b_rows.bitcast(F32), ident[:])
+        go_b_cols = keep.tile([P, GATE_TILES], BF16)
+        nc.scalar.copy(out=go_b_cols[:].bitcast(F32), in_=go_b_bank[:, 0:2])
 
         w_codes = []
         w_scales = []
@@ -138,7 +140,7 @@ def tile_aurelianmemorycore_pb_s_kernel(tc, h, gated_mem, go_w, go_b, out_w, out
                 out=gate[:, t, :],
                 in_=acc[:],
                 func=mybir.ActivationFunctionType.Sigmoid,
-                bias=go_b_f32[:, t : t + 1],
+                bias=go_b_cols[:, t : t + 1],
                 scale=1.0,
             )
 

@@ -19,19 +19,28 @@ TOKEN_TILES = TOKENS // P
 GATE_TILES = M // P
 UNIT = 1024
 BLOCKS = 4
+SPREAD = 32
 
 FLOPS = 2 * TOKENS * (D + M) * M + 2 * TOKENS * M * D
 
 
-def transpose_and_quantise(nc, psum, ident, copy, rows, grouped, codes, scales):
+def transpose(nc, psum, ident, rows):
     words = rows.bitcast(F32)
-    bank = psum.tile([P, BLOCKS, P], F32, tag="bank")
-    for b in range(BLOCKS):
+    blocks = words.shape[1] // P
+    bank = psum.tile([P, blocks, P], F32, tag="bank")
+    for b in range(blocks):
         nc.tensor.transpose(bank[:, b, :], words[:, b * P : (b + 1) * P], ident)
+    return bank
+
+
+def move_out(copy, bank, grouped):
     copy(
-        out=grouped.bitcast(F32).rearrange("q (a c u) -> q a c u", a=2, u=2),
+        out=grouped.bitcast(F32).rearrange("q (a c u) -> q a c u", c=P, u=2),
         in_=bank[:].rearrange("q (a u) c -> q a c u", u=2),
     )
+
+
+def quantise(nc, grouped, codes, scales):
     nc.vector.quantize_mx(out=codes.bitcast(FP8X4), scales=scales, in_=grouped)
 
 
@@ -42,24 +51,22 @@ def tile_aurelianmemorycore_pb_s_kernel(tc, h, gated_mem, go_w, go_b, out_w, out
         psum = ctx.enter_context(tc.psum_pool(name="psum", bufs=8))
         ctx.enter_context(tc.manual_schedule())
 
-        bias_rows = keep.tile([P, D + GATE_TILES * P // 2], BF16)
-        nc.vector.memset(bias_rows[:].bitcast(I32), 0)
-        out_b_row = bias_rows[:, 0:D]
-        go_b_rows = bias_rows[:, D : D + 2 * P]
-        nc.scalar.dma_start(out=go_b_rows[0:2, :], in_=go_b.rearrange("(u k) -> u k", u=2))
-
+        out_b_rows = keep.tile([P, D], BF16)
+        nc.sync.dma_start(out=out_b_rows[0:SPREAD, :], in_=out_b.partition_broadcast(SPREAD))
         h_rows = keep.tile([P, UNIT], BF16)
         g_rows = keep.tile([P, UNIT], BF16)
-        nc.sync.dma_start(out=h_rows[:], in_=h.flatten_outer_dims().rearrange("(p j) d -> p (j d)", j=TOKEN_TILES))
-        nc.sync.dma_start(out=out_b_row[0:1, :], in_=out_b.rearrange("(o d) -> o d", o=1))
-        nc.sync.dma_start(
-            out=g_rows[:], in_=gated_mem.flatten_outer_dims().rearrange("(p j) d -> p (j d)", j=TOKEN_TILES)
-        )
+        for rows, source in ((h_rows, h), (g_rows, gated_mem)):
+            nc.sync.dma_start(out=rows[:], in_=source.flatten_outer_dims().rearrange("(p j) d -> p (j d)", j=TOKEN_TILES))
         go_w_tiles = go_w.rearrange("(u p e) k -> u e p k", u=2, e=2)
         w_rows = []
         for t in range(GATE_TILES):
             rows = keep.tile([P, UNIT], BF16, name="w_rows%d" % t)
-            nc.sync.dma_start(out=rows[:], in_=go_w_tiles[t // 2, t % 2])
+            if t < GATE_TILES - 1:
+                nc.sync.dma_start(out=rows[:], in_=go_w_tiles[t // 2, t % 2])
+            else:
+                for c in range(2):
+                    ks = slice(c * UNIT // 2, (c + 1) * UNIT // 2)
+                    nc.sync.dma_start(out=rows[:, ks], in_=go_w_tiles[t // 2, t % 2][:, ks])
             w_rows.append(rows)
         out_w_tiles = out_w.rearrange("(r p) m -> p r m", p=P)
         o_rows = []
@@ -70,107 +77,147 @@ def tile_aurelianmemorycore_pb_s_kernel(tc, h, gated_mem, go_w, go_b, out_w, out
             )
             o_rows.append(rows)
 
-        ones = keep.tile([P, P], BF16)
-        nc.vector.memset(ones[:], 1.0)
+        go_b_rows = keep.tile([P, 2 * P], BF16)
+        nc.vector.memset(go_b_rows[:].bitcast(I32), 0)
+        nc.scalar.dma_start(out=go_b_rows[0:2, :], in_=go_b.rearrange("(u k) -> u k", u=2))
+
+        nc.vector.memset(out_b_rows[32:64, :].bitcast(I32), 0)
+        nc.vector.memset(out_b_rows[64:128, :].bitcast(I32), 0)
+        spread = keep.tile([P, P], BF16)
+        nc.vector.memset(spread[:], 1.0 / SPREAD)
         ident = keep.tile([P, P], F32)
         masks.make_identity(nc, ident[:])
         warm = keep.tile([P, 1], F32)
         nc.vector.memset(warm[:], 0.0)
         nc.scalar.activation(out=warm[:], in_=warm[:], func=mybir.ActivationFunctionType.Sigmoid)
 
+        out_b_bank = psum.tile([P, D], F32, tag="bank")
+        nc.tensor.matmul(out=out_b_bank[:], lhsT=spread[:], rhs=out_b_rows[:], start=True, stop=True)
+        residual = keep.tile([P, TOKEN_TILES, D], F32)
+        for j in range(TOKEN_TILES):
+            nc.vector.tensor_tensor(
+                out=residual[:, j, :], in0=h_rows[:, j * D : (j + 1) * D], in1=out_b_bank[:], op=mybir.AluOpType.add
+            )
 
         x_grouped = []
         x_codes = []
         x_scales = []
-        residual = keep.tile([P, TOKEN_TILES, D], F32)
         for c, rows in enumerate((h_rows, g_rows)):
-            if c == 1:
-                out_b_bank = psum.tile([P, D], F32, tag="bank")
-                nc.tensor.matmul(out=out_b_bank[:], lhsT=ones[:], rhs=out_b_row, start=True, stop=True)
-                for j in range(TOKEN_TILES):
-                    nc.vector.tensor_tensor(
-                        out=residual[:, j, :], in0=h_rows[:, j * D : (j + 1) * D], in1=out_b_bank[:], op=mybir.AluOpType.add
-                    )
             grouped = keep.tile([P, UNIT], BF16, name="x_grouped%d" % c, align_bytes=64)
             codes = keep.tile([P, TOKENS], U32, name="x_codes%d" % c, align_bytes=64)
             scales = keep.tile([P, TOKENS], U8, name="x_scales%d" % c, align_bytes=64)
-            transpose_and_quantise(nc, psum, ident[:], nc.scalar.copy, rows[:], grouped[:], codes[:], scales[:])
+            bank = transpose(nc, psum, ident[:], rows[:])
+            move_out(nc.scalar.copy, bank, grouped[:])
+            quantise(nc, grouped[:], codes[:], scales[:])
             x_grouped.append(grouped)
             x_codes.append(codes)
             x_scales.append(scales)
         g_grouped = x_grouped[1]
 
-        go_b_bank = psum.tile([P, P], F32, tag="bank")
-        nc.tensor.transpose(go_b_bank[:], go_b_rows.bitcast(F32), ident[:])
-        go_b_cols = keep.tile([P, GATE_TILES], BF16)
-        nc.scalar.copy(out=go_b_cols[:].bitcast(F32), in_=go_b_bank[:, 0:2])
-
+        w_grouped = []
         w_codes = []
         w_scales = []
         for t in range(GATE_TILES):
-            grouped = keep.tile([P, UNIT], BF16, name="w_grouped%d" % t, align_bytes=64)
-            codes = keep.tile([P, 2 * P], U32, name="w_codes%d" % t, align_bytes=64)
-            scales = keep.tile([P, 2 * P], U8, name="w_scales%d" % t, align_bytes=64)
-            transpose_and_quantise(nc, psum, ident[:], nc.scalar.copy, w_rows[t][:], grouped[:], codes[:], scales[:])
-            w_codes.append(codes)
-            w_scales.append(scales)
+            w_grouped.append(keep.tile([P, UNIT], BF16, name="w_grouped%d" % t, align_bytes=64))
+            w_codes.append(keep.tile([P, 2 * P], U32, name="w_codes%d" % t, align_bytes=64))
+            w_scales.append(keep.tile([P, 2 * P], U8, name="w_scales%d" % t, align_bytes=64))
+        for t in range(2):
+            bank = transpose(nc, psum, ident[:], w_rows[t][:])
+            move_out(nc.scalar.copy, bank, w_grouped[t][:])
+            quantise(nc, w_grouped[t][:], w_codes[t][:], w_scales[t][:])
+            if t == 0:
+                go_b_bank = psum.tile([P, P], F32, tag="bank")
+                nc.tensor.transpose(go_b_bank[:], go_b_rows[:].bitcast(F32), ident[:])
+                go_b_cols = keep.tile([P, GATE_TILES], BF16)
+                nc.scalar.copy(out=go_b_cols[:].bitcast(F32), in_=go_b_bank[:, 0:2])
+        bank2 = transpose(nc, psum, ident[:], w_rows[2][:])
+        move_out(nc.scalar.copy, bank2, w_grouped[2][:])
+        halves = [slice(c * UNIT // 2, (c + 1) * UNIT // 2) for c in range(2)]
+        bank3 = [transpose(nc, psum, ident[:], w_rows[3][:, ks]) for ks in halves]
+        move_out(nc.vector.tensor_copy, bank3[0], w_grouped[3][:, halves[0]])
+        move_out(nc.scalar.copy, bank3[1], w_grouped[3][:, halves[1]])
+        quantise(nc, w_grouped[2][:], w_codes[2][:], w_scales[2][:])
+        for c in range(2):
+            cols = slice(c * P, (c + 1) * P)
+            quantise(nc, w_grouped[3][:, halves[c]], w_codes[3][:, cols], w_scales[3][:, cols])
 
-        o_codes = keep.tile([P, D], U32, align_bytes=64)
-        o_scales = keep.tile([P, D], U8, align_bytes=64)
+        o_grouped = []
+        o_codes = []
+        o_scales = []
         for half in range(2):
-            grouped = keep.tile([P, UNIT], BF16, name="o_grouped%d" % half, align_bytes=64)
-            cols = slice(half * 2 * P, (half + 1) * 2 * P)
-            copy = nc.scalar.copy if half == 0 else nc.vector.tensor_copy
-            transpose_and_quantise(nc, psum, ident[:], copy, o_rows[half][:], grouped[:], o_codes[:, cols], o_scales[:, cols])
+            o_grouped.append(keep.tile([P, UNIT], BF16, name="o_grouped%d" % half, align_bytes=64))
+            o_codes.append(keep.tile([P, 2 * P], U32, name="o_codes%d" % half, align_bytes=64))
+            o_scales.append(keep.tile([P, 2 * P], U8, name="o_scales%d" % half, align_bytes=64))
 
         gate = keep.tile([P, GATE_TILES, TOKENS], F32)
-        for t in range(GATE_TILES):
-            acc = psum.tile([P, TOKENS], F32, tag="bank")
+        acc = [psum.tile([P, TOKENS], F32, name="acc%d" % t, tag="bank") for t in range(GATE_TILES)]
+
+        def gate_tile(t, j):
+            cols = slice(j * P, (j + 1) * P)
             for c in range(2):
                 nc.tensor.matmul_mx(
-                    out=acc[:],
+                    out=acc[t][:, cols],
                     lhsT=w_codes[t][:, c * P : (c + 1) * P].bitcast(FP8X4),
                     lhsT_scale=w_scales[t][:, c * P : (c + 1) * P],
-                    rhs=x_codes[c][:].bitcast(FP8X4),
-                    rhs_scale=x_scales[c][:],
+                    rhs=x_codes[c][:, cols].bitcast(FP8X4),
+                    rhs_scale=x_scales[c][:, cols],
                     start=(c == 0),
                     stop=(c == 1),
                 )
             nc.scalar.activation(
-                out=gate[:, t, :],
-                in_=acc[:],
+                out=gate[:, t, cols],
+                in_=acc[t][:, cols],
                 func=mybir.ActivationFunctionType.Sigmoid,
                 bias=go_b_cols[:, t : t + 1],
                 scale=1.0,
             )
 
-        out_acc = []
+        gated = []
+        gated_codes = []
+        gated_scales = []
         for j in range(TOKEN_TILES):
-            cols = slice(j * P, (j + 1) * P)
-            gated = keep.tile([P, P * PACK], BF16, name="gated%d" % j, align_bytes=64)
+            gated.append(keep.tile([P, P * PACK], BF16, name="gated%d" % j, align_bytes=64))
+            gated_codes.append(keep.tile([P, P], U32, name="gated_codes%d" % j, align_bytes=64))
+            gated_scales.append(keep.tile([P, P], U8, name="gated_scales%d" % j, align_bytes=64))
+
+        def product(j):
             nc.vector.tensor_tensor(
-                out=gated[:].rearrange("q (c t) -> q c t", t=PACK),
-                in0=gate[:, :, cols].rearrange("q t c -> q c t"),
+                out=gated[j][:].rearrange("q (c t) -> q c t", t=PACK),
+                in0=gate[:, :, j * P : (j + 1) * P].rearrange("q t c -> q c t"),
                 in1=g_grouped[:, j * P * PACK : (j + 1) * P * PACK].rearrange("q (c t) -> q c t", t=PACK),
                 op=mybir.AluOpType.mult,
             )
-            codes = keep.tile([P, P], U32, name="gated_codes%d" % j, align_bytes=64)
-            scales = keep.tile([P, P], U8, name="gated_scales%d" % j, align_bytes=64)
-            nc.vector.quantize_mx(out=codes[:].bitcast(FP8X4), scales=scales[:], in_=gated[:])
-            acc = psum.tile([P, D], F32, tag="bank")
-            nc.tensor.matmul_mx(
-                out=acc[:],
-                lhsT=codes[:].bitcast(FP8X4),
-                lhsT_scale=scales[:],
-                rhs=o_codes[:].bitcast(FP8X4),
-                rhs_scale=o_scales[:],
-                start=True,
-                stop=True,
-            )
-            out_acc.append(acc)
+
+        for t in range(GATE_TILES):
+            gate_tile(t, 0)
+        product(0)
+        bank = transpose(nc, psum, ident[:], o_rows[0][:])
+        move_out(nc.scalar.copy, bank, o_grouped[0][:])
+        quantise(nc, o_grouped[0][:], o_codes[0][:], o_scales[0][:])
+        for t in range(GATE_TILES):
+            gate_tile(t, 1)
+        quantise(nc, gated[0][:], gated_codes[0][:], gated_scales[0][:])
+        product(1)
+        bank = transpose(nc, psum, ident[:], o_rows[1][:])
+        move_out(nc.scalar.copy, bank, o_grouped[1][:])
+        quantise(nc, o_grouped[1][:], o_codes[1][:], o_scales[1][:])
+        quantise(nc, gated[1][:], gated_codes[1][:], gated_scales[1][:])
 
         out_rows = out.flatten_outer_dims().rearrange("(p j) d -> p j d", j=TOKEN_TILES)
         for j in range(TOKEN_TILES):
-            result = keep.tile([P, D], F32, name="result%d" % j)
-            nc.vector.tensor_tensor(out=result[:], in0=out_acc[j][:], in1=residual[:, j, :], op=mybir.AluOpType.add)
-            nc.sync.dma_start(out=out_rows[:, j, :], in_=result[:])
+            for half in range(2):
+                cols = slice(half * 2 * P, (half + 1) * 2 * P)
+                quarter = psum.tile([P, 2 * P], F32, name="quarter%d%d" % (j, half), tag="bank")
+                nc.tensor.matmul_mx(
+                    out=quarter[:],
+                    lhsT=gated_codes[j][:].bitcast(FP8X4),
+                    lhsT_scale=gated_scales[j][:],
+                    rhs=o_codes[half][:].bitcast(FP8X4),
+                    rhs_scale=o_scales[half][:],
+                    start=True,
+                    stop=True,
+                )
+                result = keep.tile([P, 2 * P], F32, name="result%d%d" % (j, half))
+                nc.vector.tensor_tensor(out=result[:], in0=quarter[:], in1=residual[:, j, cols], op=mybir.AluOpType.add)
+                queue = nc.sync if half == 0 else nc.scalar
+                queue.dma_start(out=out_rows[:, j, cols], in_=result[:])

@@ -81,6 +81,8 @@ def tile_aurelianmemorycore_pb_s_kernel(tc, h, gated_mem, go_w, go_b, out_w, out
         nc.vector.memset(go_b_rows[:].bitcast(I32), 0)
         nc.scalar.dma_start(out=go_b_rows[0:2, :], in_=go_b.rearrange("(u k) -> u k", u=2))
 
+        ticks = keep.tile([P, P], F32)
+        nc.vector.memset(ticks[:], 0.0)
         nc.vector.memset(out_b_rows[32:64, :].bitcast(I32), 0)
         nc.vector.memset(out_b_rows[64:128, :].bitcast(I32), 0)
         spread = keep.tile([P, P], BF16)
@@ -90,6 +92,13 @@ def tile_aurelianmemorycore_pb_s_kernel(tc, h, gated_mem, go_w, go_b, out_w, out
         warm = keep.tile([P, 1], F32)
         nc.vector.memset(warm[:], 0.0)
         nc.scalar.activation(out=warm[:], in_=warm[:], func=mybir.ActivationFunctionType.Sigmoid)
+
+        def keep_clock_up():
+            idle_bank = psum.tile([P, P], F32, tag="bank")
+            nc.tensor.matmul(out=idle_bank[:], lhsT=ticks[:], rhs=ticks[:], start=True, stop=True)
+
+        for i in range(3):
+            keep_clock_up()
 
         out_b_bank = psum.tile([P, D], F32, tag="bank")
         nc.tensor.matmul(out=out_b_bank[:], lhsT=spread[:], rhs=out_b_rows[:], start=True, stop=True)
@@ -112,6 +121,7 @@ def tile_aurelianmemorycore_pb_s_kernel(tc, h, gated_mem, go_w, go_b, out_w, out
             x_grouped.append(grouped)
             x_codes.append(codes)
             x_scales.append(scales)
+        keep_clock_up()
         g_grouped = x_grouped[1]
 
         w_grouped = []
@@ -130,6 +140,7 @@ def tile_aurelianmemorycore_pb_s_kernel(tc, h, gated_mem, go_w, go_b, out_w, out
                 nc.tensor.transpose(go_b_bank[:], go_b_rows[:].bitcast(F32), ident[:])
                 go_b_cols = keep.tile([P, GATE_TILES], BF16)
                 nc.scalar.copy(out=go_b_cols[:].bitcast(F32), in_=go_b_bank[:, 0:2])
+        keep_clock_up()
         bank2 = transpose(nc, psum, ident[:], w_rows[2][:])
         move_out(nc.scalar.copy, bank2, w_grouped[2][:])
         halves = [slice(c * UNIT // 2, (c + 1) * UNIT // 2) for c in range(2)]

@@ -24,65 +24,46 @@ SPREAD = 32
 FLOPS = 2 * TOKENS * (D + M) * M + 2 * TOKENS * M * D
 
 
-def transpose(nc, psum, ident, rows):
-    words = rows.bitcast(F32)
-    blocks = words.shape[1] // P
-    bank = psum.tile([P, blocks, P], F32, tag="bank")
-    for b in range(blocks):
-        nc.tensor.transpose(bank[:, b, :], words[:, b * P : (b + 1) * P], ident)
-    return bank
-
-
-def move_out(copy, bank, grouped):
-    copy(
-        out=grouped.bitcast(F32).rearrange("q (a c u) -> q a c u", c=P, u=2),
-        in_=bank[:].rearrange("q (a u) c -> q a c u", u=2),
-    )
-
-
-def quantise(nc, grouped, codes, scales):
-    nc.vector.quantize_mx(out=codes.bitcast(FP8X4), scales=scales, in_=grouped)
-
-
 def tile_aurelianmemorycore_pb_s_kernel(tc, h, gated_mem, go_w, go_b, out_w, out_b, out):
     nc = tc.nc
     with ExitStack() as ctx:
         keep = ctx.enter_context(tc.tile_pool(name="keep", bufs=1))
         psum = ctx.enter_context(tc.psum_pool(name="psum", bufs=8))
         ctx.enter_context(tc.manual_schedule())
+        on_scalar = nc.scalar.copy
+        on_vector = nc.vector.tensor_copy
 
-        out_b_rows = keep.tile([P, D], BF16)
-        nc.sync.dma_start(out=out_b_rows[0:SPREAD, :], in_=out_b.partition_broadcast(SPREAD))
-        h_rows = keep.tile([P, UNIT], BF16)
-        g_rows = keep.tile([P, UNIT], BF16)
-        for rows, source in ((h_rows, h), (g_rows, gated_mem)):
-            nc.sync.dma_start(out=rows[:], in_=source.flatten_outer_dims().rearrange("(p j) d -> p (j d)", j=TOKEN_TILES))
-        go_w_tiles = go_w.rearrange("(u p e) k -> u e p k", u=2, e=2)
-        w_rows = []
-        for t in range(GATE_TILES):
-            rows = keep.tile([P, UNIT], BF16, name="w_rows%d" % t)
-            if t < GATE_TILES - 1:
-                nc.sync.dma_start(out=rows[:], in_=go_w_tiles[t // 2, t % 2])
-            else:
-                for c in range(2):
-                    ks = slice(c * UNIT // 2, (c + 1) * UNIT // 2)
-                    nc.sync.dma_start(out=rows[:, ks], in_=go_w_tiles[t // 2, t % 2][:, ks])
-            w_rows.append(rows)
-        out_w_tiles = out_w.rearrange("(r p) m -> p r m", p=P)
-        o_rows = []
-        for half in range(2):
-            rows = keep.tile([P, UNIT], BF16, name="o_rows%d" % half)
-            nc.sync.dma_start(
-                out=rows[:].rearrange("p (r m) -> p r m", r=2), in_=out_w_tiles[:, 2 * half : 2 * half + 2, :]
+        def operand(name, units):
+            return (
+                keep.tile([P, units * UNIT], BF16, name=name + "_rows", align_bytes=64),
+                keep.tile([P, units * UNIT], BF16, name=name + "_grouped", align_bytes=64),
+                keep.tile([P, units * UNIT // PACK], U32, name=name + "_codes", align_bytes=64),
+                keep.tile([P, units * UNIT // PACK], U8, name=name + "_scales", align_bytes=64),
             )
-            o_rows.append(rows)
 
-        go_b_rows = keep.tile([P, 2 * P], BF16)
-        nc.vector.memset(go_b_rows[:].bitcast(I32), 0)
-        nc.scalar.dma_start(out=go_b_rows[0:2, :], in_=go_b.rearrange("(u k) -> u k", u=2))
+        x = [operand("h", 1), operand("g", 1)]
+        w = [operand("w%d" % t, 1) for t in range(GATE_TILES)]
+        o = operand("o", 2)
 
         ticks = keep.tile([P, P], F32)
         nc.vector.memset(ticks[:], 0.0)
+        out_b_rows = keep.tile([P, D], BF16)
+        nc.sync.dma_start(out=out_b_rows[0:SPREAD, :], in_=out_b.partition_broadcast(SPREAD))
+        go_b_rows = keep.tile([P, 2 * P], BF16)
+        nc.vector.memset(go_b_rows[:].bitcast(I32), 0)
+        nc.scalar.dma_start(out=go_b_rows[0:2, :], in_=go_b.rearrange("(u k) -> u k", u=2))
+        halves = [slice(c * UNIT // 2, (c + 1) * UNIT // 2) for c in range(2)]
+        go_w_tiles = go_w.rearrange("(u p e) k -> u e p k", u=2, e=2)
+        out_w_tiles = out_w.rearrange("(r p) m -> p r m", p=P)
+        nc.sync.dma_start(out=x[0][0][:], in_=h.flatten_outer_dims().rearrange("(p j) d -> p (j d)", j=TOKEN_TILES))
+        nc.sync.dma_start(out=x[1][0][:], in_=gated_mem.flatten_outer_dims().rearrange("(p j) d -> p (j d)", j=TOKEN_TILES))
+        nc.sync.dma_start(out=w[0][0][:], in_=go_w_tiles[0, 0])
+        nc.sync.dma_start(out=w[1][0][:], in_=go_w_tiles[0, 1])
+        nc.sync.dma_start(out=w[2][0][:], in_=go_w_tiles[1, 0])
+        nc.sync.dma_start(out=w[3][0][:, halves[0]], in_=go_w_tiles[1, 1][:, halves[0]])
+        nc.sync.dma_start(out=w[3][0][:, halves[1]], in_=go_w_tiles[1, 1][:, halves[1]])
+        nc.sync.dma_start(out=o[0][:, 0 * UNIT : 1 * UNIT].rearrange("p (r m) -> p r m", r=2), in_=out_w_tiles[:, 0 : 2, :])
+        nc.sync.dma_start(out=o[0][:, 1 * UNIT : 2 * UNIT].rearrange("p (r m) -> p r m", r=2), in_=out_w_tiles[:, 2 : 4, :])
         nc.vector.memset(out_b_rows[32:64, :].bitcast(I32), 0)
         nc.vector.memset(out_b_rows[64:128, :].bitcast(I32), 0)
         spread = keep.tile([P, P], BF16)
@@ -93,142 +74,184 @@ def tile_aurelianmemorycore_pb_s_kernel(tc, h, gated_mem, go_w, go_b, out_w, out
         nc.vector.memset(warm[:], 0.0)
         nc.scalar.activation(out=warm[:], in_=warm[:], func=mybir.ActivationFunctionType.Sigmoid)
 
+        def transpose(rows):
+            words = rows.bitcast(F32)
+            blocks = words.shape[1] // P
+            bank = psum.tile([P, blocks, P], F32, tag="bank")
+            for b in range(blocks):
+                nc.tensor.transpose(bank[:, b, :], words[:, b * P : (b + 1) * P], ident[:])
+            return bank
+
+        def move_out(copy, bank, grouped):
+            copy(
+                out=grouped.bitcast(F32).rearrange("q (a c u) -> q a c u", c=P, u=2),
+                in_=bank[:].rearrange("q (a u) c -> q a c u", u=2),
+            )
+
+        def quantise(grouped, codes, scales):
+            nc.vector.quantize_mx(out=codes.bitcast(FP8X4), scales=scales, in_=grouped)
+
+        def quantise_all(operand_tiles):
+            quantise(operand_tiles[1][:], operand_tiles[2][:], operand_tiles[3][:])
+
         def keep_clock_up():
             idle_bank = psum.tile([P, P], F32, tag="bank")
             nc.tensor.matmul(out=idle_bank[:], lhsT=ticks[:], rhs=ticks[:], start=True, stop=True)
 
-        for i in range(3):
-            keep_clock_up()
+        def keep_clock_up_mx(n):
+            idle_bank = psum.tile([P, TOKENS], F32, tag="bank")
+            for i in range(n):
+                nc.tensor.matmul_mx(
+                    out=idle_bank[:],
+                    lhsT=x[0][2][:, 0:P].bitcast(FP8X4),
+                    lhsT_scale=x[0][3][:, 0:P],
+                    rhs=x[0][2][:].bitcast(FP8X4),
+                    rhs_scale=x[0][3][:],
+                    start=True,
+                    stop=True,
+                )
 
-        out_b_bank = psum.tile([P, D], F32, tag="bank")
-        nc.tensor.matmul(out=out_b_bank[:], lhsT=spread[:], rhs=out_b_rows[:], start=True, stop=True)
+        def spread_out_b():
+            bank = psum.tile([P, D], F32, tag="bank")
+            nc.tensor.matmul(out=bank[:], lhsT=spread[:], rhs=out_b_rows[:], start=True, stop=True)
+            return bank
+
         residual = keep.tile([P, TOKEN_TILES, D], F32)
-        for j in range(TOKEN_TILES):
+
+        def add_residual(j, bank):
             nc.vector.tensor_tensor(
-                out=residual[:, j, :], in0=h_rows[:, j * D : (j + 1) * D], in1=out_b_bank[:], op=mybir.AluOpType.add
+                out=residual[:, j, :], in0=x[0][0][:, j * D : (j + 1) * D], in1=bank[:], op=mybir.AluOpType.add
             )
 
-        x_grouped = []
-        x_codes = []
-        x_scales = []
-        for c, rows in enumerate((h_rows, g_rows)):
-            grouped = keep.tile([P, UNIT], BF16, name="x_grouped%d" % c, align_bytes=64)
-            codes = keep.tile([P, TOKENS], U32, name="x_codes%d" % c, align_bytes=64)
-            scales = keep.tile([P, TOKENS], U8, name="x_scales%d" % c, align_bytes=64)
-            bank = transpose(nc, psum, ident[:], rows[:])
-            move_out(nc.scalar.copy, bank, grouped[:])
-            quantise(nc, grouped[:], codes[:], scales[:])
-            x_grouped.append(grouped)
-            x_codes.append(codes)
-            x_scales.append(scales)
-        keep_clock_up()
-        g_grouped = x_grouped[1]
-
-        w_grouped = []
-        w_codes = []
-        w_scales = []
-        for t in range(GATE_TILES):
-            w_grouped.append(keep.tile([P, UNIT], BF16, name="w_grouped%d" % t, align_bytes=64))
-            w_codes.append(keep.tile([P, 2 * P], U32, name="w_codes%d" % t, align_bytes=64))
-            w_scales.append(keep.tile([P, 2 * P], U8, name="w_scales%d" % t, align_bytes=64))
-        for t in range(2):
-            bank = transpose(nc, psum, ident[:], w_rows[t][:])
-            move_out(nc.scalar.copy, bank, w_grouped[t][:])
-            quantise(nc, w_grouped[t][:], w_codes[t][:], w_scales[t][:])
-            if t == 0:
-                go_b_bank = psum.tile([P, P], F32, tag="bank")
-                nc.tensor.transpose(go_b_bank[:], go_b_rows[:].bitcast(F32), ident[:])
-                go_b_cols = keep.tile([P, GATE_TILES], BF16)
-                nc.scalar.copy(out=go_b_cols[:].bitcast(F32), in_=go_b_bank[:, 0:2])
-        keep_clock_up()
-        bank2 = transpose(nc, psum, ident[:], w_rows[2][:])
-        move_out(nc.scalar.copy, bank2, w_grouped[2][:])
-        halves = [slice(c * UNIT // 2, (c + 1) * UNIT // 2) for c in range(2)]
-        bank3 = [transpose(nc, psum, ident[:], w_rows[3][:, ks]) for ks in halves]
-        move_out(nc.vector.tensor_copy, bank3[0], w_grouped[3][:, halves[0]])
-        move_out(nc.scalar.copy, bank3[1], w_grouped[3][:, halves[1]])
-        quantise(nc, w_grouped[2][:], w_codes[2][:], w_scales[2][:])
-        for c in range(2):
-            cols = slice(c * P, (c + 1) * P)
-            quantise(nc, w_grouped[3][:, halves[c]], w_codes[3][:, cols], w_scales[3][:, cols])
-
-        o_grouped = []
-        o_codes = []
-        o_scales = []
-        for half in range(2):
-            o_grouped.append(keep.tile([P, UNIT], BF16, name="o_grouped%d" % half, align_bytes=64))
-            o_codes.append(keep.tile([P, 2 * P], U32, name="o_codes%d" % half, align_bytes=64))
-            o_scales.append(keep.tile([P, 2 * P], U8, name="o_scales%d" % half, align_bytes=64))
-
-        gate = keep.tile([P, GATE_TILES, TOKENS], F32)
-        acc = [psum.tile([P, TOKENS], F32, name="acc%d" % t, tag="bank") for t in range(GATE_TILES)]
-
-        def gate_tile(t, j):
-            cols = slice(j * P, (j + 1) * P)
+        def gate_passes(t, first, end):
+            acc = psum.tile([P, end - first], F32, tag="bank")
             for c in range(2):
                 nc.tensor.matmul_mx(
-                    out=acc[t][:, cols],
-                    lhsT=w_codes[t][:, c * P : (c + 1) * P].bitcast(FP8X4),
-                    lhsT_scale=w_scales[t][:, c * P : (c + 1) * P],
-                    rhs=x_codes[c][:, cols].bitcast(FP8X4),
-                    rhs_scale=x_scales[c][:, cols],
+                    out=acc[:],
+                    lhsT=w[t][2][:, c * P : (c + 1) * P].bitcast(FP8X4),
+                    lhsT_scale=w[t][3][:, c * P : (c + 1) * P],
+                    rhs=x[c][2][:, first:end].bitcast(FP8X4),
+                    rhs_scale=x[c][3][:, first:end],
                     start=(c == 0),
                     stop=(c == 1),
                 )
+            return acc
+
+        gate = keep.tile([P, GATE_TILES, TOKENS], F32)
+
+        def sigmoid(t, first, end, acc):
             nc.scalar.activation(
-                out=gate[:, t, cols],
-                in_=acc[t][:, cols],
+                out=gate[:, t, first:end],
+                in_=acc[:],
                 func=mybir.ActivationFunctionType.Sigmoid,
                 bias=go_b_cols[:, t : t + 1],
                 scale=1.0,
             )
 
-        gated = []
-        gated_codes = []
-        gated_scales = []
-        for j in range(TOKEN_TILES):
-            gated.append(keep.tile([P, P * PACK], BF16, name="gated%d" % j, align_bytes=64))
-            gated_codes.append(keep.tile([P, P], U32, name="gated_codes%d" % j, align_bytes=64))
-            gated_scales.append(keep.tile([P, P], U8, name="gated_scales%d" % j, align_bytes=64))
+        gated = keep.tile([P, TOKENS * PACK], BF16, align_bytes=64)
+        gated_codes = keep.tile([P, TOKENS], U32, align_bytes=64)
+        gated_scales = keep.tile([P, TOKENS], U8, align_bytes=64)
 
-        def product(j):
+        def product(first, end):
+            values = slice(first * PACK, end * PACK)
             nc.vector.tensor_tensor(
-                out=gated[j][:].rearrange("q (c t) -> q c t", t=PACK),
-                in0=gate[:, :, j * P : (j + 1) * P].rearrange("q t c -> q c t"),
-                in1=g_grouped[:, j * P * PACK : (j + 1) * P * PACK].rearrange("q (c t) -> q c t", t=PACK),
+                out=gated[:, values].rearrange("q (c t) -> q c t", t=PACK),
+                in0=gate[:, :, first:end].rearrange("q t c -> q c t"),
+                in1=x[1][1][:, values].rearrange("q (c t) -> q c t", t=PACK),
                 op=mybir.AluOpType.mult,
             )
 
-        for t in range(GATE_TILES):
-            gate_tile(t, 0)
-        product(0)
-        bank = transpose(nc, psum, ident[:], o_rows[0][:])
-        move_out(nc.scalar.copy, bank, o_grouped[0][:])
-        quantise(nc, o_grouped[0][:], o_codes[0][:], o_scales[0][:])
-        for t in range(GATE_TILES):
-            gate_tile(t, 1)
-        quantise(nc, gated[0][:], gated_codes[0][:], gated_scales[0][:])
-        product(1)
-        bank = transpose(nc, psum, ident[:], o_rows[1][:])
-        move_out(nc.scalar.copy, bank, o_grouped[1][:])
-        quantise(nc, o_grouped[1][:], o_codes[1][:], o_scales[1][:])
-        quantise(nc, gated[1][:], gated_codes[1][:], gated_scales[1][:])
+        def quantise_gated(j):
+            cols = slice(j * P, (j + 1) * P)
+            quantise(gated[:, j * P * PACK : (j + 1) * P * PACK], gated_codes[:, cols], gated_scales[:, cols])
 
         out_rows = out.flatten_outer_dims().rearrange("(p j) d -> p j d", j=TOKEN_TILES)
-        for j in range(TOKEN_TILES):
-            for half in range(2):
-                cols = slice(half * 2 * P, (half + 1) * 2 * P)
-                quarter = psum.tile([P, 2 * P], F32, name="quarter%d%d" % (j, half), tag="bank")
-                nc.tensor.matmul_mx(
-                    out=quarter[:],
-                    lhsT=gated_codes[j][:].bitcast(FP8X4),
-                    lhsT_scale=gated_scales[j][:],
-                    rhs=o_codes[half][:].bitcast(FP8X4),
-                    rhs_scale=o_scales[half][:],
-                    start=True,
-                    stop=True,
-                )
-                result = keep.tile([P, 2 * P], F32, name="result%d%d" % (j, half))
-                nc.vector.tensor_tensor(out=result[:], in0=quarter[:], in1=residual[:, j, cols], op=mybir.AluOpType.add)
-                queue = nc.sync if half == 0 else nc.scalar
-                queue.dma_start(out=out_rows[:, j, cols], in_=result[:])
+
+        def out_pass(j, first, end):
+            acc = psum.tile([P, end - first], F32, tag="bank")
+            nc.tensor.matmul_mx(
+                out=acc[:],
+                lhsT=gated_codes[:, j * P : (j + 1) * P].bitcast(FP8X4),
+                lhsT_scale=gated_scales[:, j * P : (j + 1) * P],
+                rhs=o[2][:, first:end].bitcast(FP8X4),
+                rhs_scale=o[3][:, first:end],
+                start=True,
+                stop=True,
+            )
+            return acc
+
+        def finish(j, first, end, acc, queue):
+            result = keep.tile([P, end - first], F32, name="result%d_%d" % (j, first))
+            nc.vector.tensor_tensor(out=result[:], in0=acc[:], in1=residual[:, j, first:end], op=mybir.AluOpType.add)
+            queue.dma_start(out=out_rows[:, j, first:end], in_=result[:])
+
+        keep_clock_up()
+        keep_clock_up()
+        keep_clock_up()
+        out_b_bank = spread_out_b()
+        add_residual(0, out_b_bank)
+        add_residual(1, out_b_bank)
+        bank_h = transpose(x[0][0][:])
+        move_out(on_scalar, bank_h, x[0][1][:])
+        quantise(x[0][1][:], x[0][2][:], x[0][3][:])
+        bank_g = transpose(x[1][0][:])
+        move_out(on_scalar, bank_g, x[1][1][:])
+        quantise(x[1][1][:], x[1][2][:], x[1][3][:])
+        keep_clock_up()
+        bank_w0 = transpose(w[0][0][:])
+        move_out(on_scalar, bank_w0, w[0][1][:])
+        quantise(w[0][1][:], w[0][2][:], w[0][3][:])
+        bank_w1 = transpose(w[1][0][:])
+        move_out(on_scalar, bank_w1, w[1][1][:])
+        quantise(w[1][1][:], w[1][2][:], w[1][3][:])
+        go_b_bank = psum.tile([P, P], F32, tag="bank")
+        nc.tensor.transpose(go_b_bank[:], go_b_rows[:].bitcast(F32), ident[:])
+        go_b_cols = keep.tile([P, GATE_TILES], BF16)
+        nc.scalar.copy(out=go_b_cols[:].bitcast(F32), in_=go_b_bank[:, 0:2])
+        keep_clock_up()
+        bank_w2 = transpose(w[2][0][:])
+        move_out(on_scalar, bank_w2, w[2][1][:])
+        bank_w3a = transpose(w[3][0][:, 0:512])
+        bank_w3b = transpose(w[3][0][:, 512:1024])
+        move_out(on_vector, bank_w3a, w[3][1][:, 0:512])
+        move_out(on_scalar, bank_w3b, w[3][1][:, 512:1024])
+        quantise(w[2][1][:], w[2][2][:], w[2][3][:])
+        quantise(w[3][1][:], w[3][2][:], w[3][3][:])
+        acc_00 = gate_passes(0, 0, P)
+        sigmoid(0, 0, P, acc_00)
+        acc_10 = gate_passes(1, 0, P)
+        sigmoid(1, 0, P, acc_10)
+        bank_o0a = transpose(o[0][:, 0:512])
+        bank_o0b = transpose(o[0][:, 512:1024])
+        move_out(on_scalar, bank_o0b, o[1][:, 512:1024])
+        acc_20 = gate_passes(2, 0, P)
+        sigmoid(2, 0, P, acc_20)
+        acc_30 = gate_passes(3, 0, P)
+        sigmoid(3, 0, P, acc_30)
+        move_out(on_vector, bank_o0a, o[1][:, 0:512])
+        quantise(o[1][:, 0:1024], o[2][:, 0:256], o[3][:, 0:256])
+        acc_01 = gate_passes(0, P, TOKENS)
+        sigmoid(0, P, TOKENS, acc_01)
+        acc_11 = gate_passes(1, P, TOKENS)
+        sigmoid(1, P, TOKENS, acc_11)
+        acc_21 = gate_passes(2, P, TOKENS)
+        sigmoid(2, P, TOKENS, acc_21)
+        acc_31 = gate_passes(3, P, TOKENS)
+        sigmoid(3, P, TOKENS, acc_31)
+        product(0, 128)
+        product(128, 192)
+        quantise_gated(0)
+        product(192, 256)
+        bank_o1 = transpose(o[0][:, 1024:2048])
+        keep_clock_up_mx(2)
+        move_out(on_scalar, bank_o1, o[1][:, 1024:2048])
+        quantise(o[1][:, 1024:2048], o[2][:, 256:512], o[3][:, 256:512])
+        quantise_gated(1)
+        out_00 = out_pass(0, 0, D // 2)
+        finish(0, 0, D // 2, out_00, nc.sync)
+        out_01 = out_pass(0, D // 2, D)
+        finish(0, D // 2, D, out_01, nc.scalar)
+        out_10 = out_pass(1, 0, D // 2)
+        finish(1, 0, D // 2, out_10, nc.sync)
+        out_11 = out_pass(1, D // 2, D)
+        finish(1, D // 2, D, out_11, nc.sync)

@@ -155,9 +155,9 @@ def tile_aurelianmemorycore_pb_s_kernel(tc, h, gated_mem, go_w, go_b, out_w, out
         def product(first, end):
             values = slice(first * PACK, end * PACK)
             nc.vector.tensor_tensor(
-                out=gated[:, values].rearrange("q (c t) -> q c t", t=PACK),
-                in0=gate[:, :, first:end].rearrange("q t c -> q c t"),
-                in1=x[1][1][:, values].rearrange("q (c t) -> q c t", t=PACK),
+                out=gated[:, values].rearrange("q (c i t) -> q c t i", i=4, t=PACK),
+                in0=gate[:, :, first:end].rearrange("q t (c i) -> q c t i", i=4),
+                in1=x[1][1][:, values].rearrange("q (c i t) -> q c t i", i=4, t=PACK),
                 op=mybir.AluOpType.mult,
             )
 
@@ -250,7 +250,7 @@ def tile_aurelianmemorycore_pb_s_kernel(tc, h, gated_mem, go_w, go_b, out_w, out
         out_00 = out_pass(0, 0, D // 2)
         finish(0, 0, D // 2, out_00, nc.sync)
         out_01 = out_pass(0, D // 2, D)
-        finish(0, D // 2, D, out_01, nc.scalar)
+        finish(0, D // 2, D, out_01, nc.sync)
         out_10 = out_pass(1, 0, D // 2)
         finish(1, 0, D // 2, out_10, nc.sync)
         out_11 = out_pass(1, D // 2, D)

@@ -217,8 +217,8 @@ def tile_aurelianmemorycore_pb_s_kernel(tc, h, gated_mem, go_w, go_b, out_w, out
         move_out(on_scalar, bank_w3b, w[3][1][:, 512:1024])
         quantise(w[2][1][:], w[2][2][:], w[2][3][:])
         quantise(w[3][1][:], w[3][2][:], w[3][3][:])
-        acc_00 = gate_passes(0, 0, P)
-        sigmoid(0, 0, P, acc_00)
+        acc_0a = gate_passes(0, 0, TOKENS)
+        sigmoid(0, 0, TOKENS, acc_0a)
         acc_10 = gate_passes(1, 0, P)
         sigmoid(1, 0, P, acc_10)
         bank_o0a = transpose(o[0][:, 0:512])
@@ -230,8 +230,6 @@ def tile_aurelianmemorycore_pb_s_kernel(tc, h, gated_mem, go_w, go_b, out_w, out
         sigmoid(3, 0, P, acc_30)
         move_out(on_vector, bank_o0a, o[1][:, 0:512])
         quantise(o[1][:, 0:1024], o[2][:, 0:256], o[3][:, 0:256])
-        acc_01 = gate_passes(0, P, TOKENS)
-        sigmoid(0, P, TOKENS, acc_01)
         acc_11 = gate_passes(1, P, TOKENS)
         sigmoid(1, P, TOKENS, acc_11)
         acc_21 = gate_passes(2, P, TOKENS)

from contextlib import ExitStack

import concourse.masks as masks
import concourse.mybir as mybir

F32 = mybir.dt.float32
BF16 = mybir.dt.bfloat16
U32 = mybir.dt.uint32
I32 = mybir.dt.int32
U8 = mybir.dt.uint8
FP8X4 = mybir.dt.float8_e4m3fn_x4

P = 128
PACK = 4
TOKENS = 256
D = 512
M = 512
TOKEN_TILES = TOKENS // P
GATE_TILES = M // P
UNIT = 1024
BLOCKS = 4
SPREAD = 32

FLOPS = 2 * TOKENS * (D + M) * M + 2 * TOKENS * M * D


def tile_aurelianmemorycore_pb_s_kernel(tc, h, gated_mem, go_w, go_b, out_w, out_b, out):
    nc = tc.nc
    with ExitStack() as ctx:
        keep = ctx.enter_context(tc.tile_pool(name="keep", bufs=1))
        psum = ctx.enter_context(tc.psum_pool(name="psum", bufs=8))
        ctx.enter_context(tc.manual_schedule())
        on_scalar = nc.scalar.copy
        on_vector = nc.vector.tensor_copy

        def operand(name, units):
            return (
                keep.tile([P, units * UNIT], BF16, name=name + "_rows", align_bytes=64),
                keep.tile([P, units * UNIT], BF16, name=name + "_grouped", align_bytes=64),
                keep.tile([P, units * UNIT // PACK], U32, name=name + "_codes", align_bytes=64),
                keep.tile([P, units * UNIT // PACK], U8, name=name + "_scales", align_bytes=64),
            )

        x = [operand("h", 1), operand("g", 1)]
        w = [operand("w%d" % t, 1) for t in range(GATE_TILES)]
        o = operand("o", 2)

        ticks = keep.tile([P, P], F32)
        nc.vector.memset(ticks[:], 0.0)
        out_b_rows = keep.tile([P, D], BF16)
        nc.sync.dma_start(out=out_b_rows[0:SPREAD, :], in_=out_b.partition_broadcast(SPREAD))
        go_b_rows = keep.tile([P, 2 * P], BF16)
        nc.vector.memset(go_b_rows[:].bitcast(I32), 0)
        nc.scalar.dma_start(out=go_b_rows[0:2, :], in_=go_b.rearrange("(u k) -> u k", u=2))
        halves = [slice(c * UNIT // 2, (c + 1) * UNIT // 2) for c in range(2)]
        go_w_tiles = go_w.rearrange("(u p e) k -> u e p k", u=2, e=2)
        out_w_tiles = out_w.rearrange("(r p) m -> p r m", p=P)
        nc.sync.dma_start(out=x[0][0][:], in_=h.flatten_outer_dims().rearrange("(p j) d -> p (j d)", j=TOKEN_TILES))
        nc.sync.dma_start(out=x[1][0][:], in_=gated_mem.flatten_outer_dims().rearrange("(p j) d -> p (j d)", j=TOKEN_TILES))
        nc.sync.dma_start(out=w[0][0][:], in_=go_w_tiles[0, 0])
        nc.sync.dma_start(out=w[1][0][:], in_=go_w_tiles[0, 1])
        nc.sync.dma_start(out=w[2][0][:], in_=go_w_tiles[1, 0])
        nc.sync.dma_start(out=w[3][0][:, halves[0]], in_=go_w_tiles[1, 1][:, halves[0]])
        nc.sync.dma_start(out=w[3][0][:, halves[1]], in_=go_w_tiles[1, 1][:, halves[1]])
        nc.sync.dma_start(out=o[0][:, 0 * UNIT : 1 * UNIT].rearrange("p (r m) -> p r m", r=2), in_=out_w_tiles[:, 0 : 2, :])
        nc.sync.dma_start(out=o[0][:, 1 * UNIT : 2 * UNIT].rearrange("p (r m) -> p r m", r=2), in_=out_w_tiles[:, 2 : 4, :])
        nc.vector.memset(out_b_rows[32:64, :].bitcast(I32), 0)
        nc.vector.memset(out_b_rows[64:128, :].bitcast(I32), 0)
        spread = keep.tile([P, P], BF16)
        nc.vector.memset(spread[:], 1.0 / SPREAD)
        ident = keep.tile([P, P], F32)
        masks.make_identity(nc, ident[:])
        warm = keep.tile([P, 1], F32)
        nc.vector.memset(warm[:], 0.0)
        nc.scalar.activation(out=warm[:], in_=warm[:], func=mybir.ActivationFunctionType.Sigmoid)

        def transpose(rows):
            words = rows.bitcast(F32)
            blocks = words.shape[1] // P
            bank = psum.tile([P, blocks, P], F32, tag="bank")
            for b in range(blocks):
                nc.tensor.transpose(bank[:, b, :], words[:, b * P : (b + 1) * P], ident[:])
            return bank

        def move_out(copy, bank, grouped):
            copy(
                out=grouped.bitcast(F32).rearrange("q (a c u) -> q a c u", c=P, u=2),
                in_=bank[:].rearrange("q (a u) c -> q a c u", u=2),
            )

        def quantise(grouped, codes, scales):
            nc.vector.quantize_mx(out=codes.bitcast(FP8X4), scales=scales, in_=grouped)

        def quantise_all(operand_tiles):
            quantise(operand_tiles[1][:], operand_tiles[2][:], operand_tiles[3][:])

        def keep_clock_up():
            idle_bank = psum.tile([P, P], F32, tag="bank")
            nc.tensor.matmul(out=idle_bank[:], lhsT=ticks[:], rhs=ticks[:], start=True, stop=True)

        def keep_clock_up_mx(n):
            idle_bank = psum.tile([P, TOKENS], F32, tag="bank")
            for i in range(n):
                nc.tensor.matmul_mx(
                    out=idle_bank[:],
                    lhsT=x[0][2][:, 0:P].bitcast(FP8X4),
                    lhsT_scale=x[0][3][:, 0:P],
                    rhs=x[0][2][:].bitcast(FP8X4),
                    rhs_scale=x[0][3][:],
                    start=True,
                    stop=True,
                )

        def spread_out_b():
            bank = psum.tile([P, D], F32, tag="bank")
            nc.tensor.matmul(out=bank[:], lhsT=spread[:], rhs=out_b_rows[:], start=True, stop=True)
            return bank

        residual = keep.tile([P, TOKEN_TILES, D], F32)

        def add_residual(j, bank):
            nc.vector.tensor_tensor(
                out=residual[:, j, :], in0=x[0][0][:, j * D : (j + 1) * D], in1=bank[:], op=mybir.AluOpType.add
            )

        def gate_passes(t, first, end):
            acc = psum.tile([P, end - first], F32, tag="bank")
            for c in range(2):
                nc.tensor.matmul_mx(
                    out=acc[:],
                    lhsT=w[t][2][:, c * P : (c + 1) * P].bitcast(FP8X4),
                    lhsT_scale=w[t][3][:, c * P : (c + 1) * P],
                    rhs=x[c][2][:, first:end].bitcast(FP8X4),
                    rhs_scale=x[c][3][:, first:end],
                    start=(c == 0),
                    stop=(c == 1),
                )
            return acc

        gate = keep.tile([P, GATE_TILES, TOKENS], F32)

        def sigmoid(t, first, end, acc):
            nc.scalar.activation(
                out=gate[:, t, first:end],
                in_=acc[:],
                func=mybir.ActivationFunctionType.Sigmoid,
                bias=go_b_cols[:, t : t + 1],
                scale=1.0,
            )

        gated = keep.tile([P, TOKENS * PACK], BF16, align_bytes=64)
        gated_codes = keep.tile([P, TOKENS], U32, align_bytes=64)
        gated_scales = keep.tile([P, TOKENS], U8, align_bytes=64)

        def product(first, end):
            values = slice(first * PACK, end * PACK)
            nc.vector.tensor_tensor(
                out=gated[:, values].rearrange("q (c i t) -> q c t i", i=4, t=PACK),
                in0=gate[:, :, first:end].rearrange("q t (c i) -> q c t i", i=4),
                in1=x[1][1][:, values].rearrange("q (c i t) -> q c t i", i=4, t=PACK),
                op=mybir.AluOpType.mult,
            )

        def quantise_gated(j):
            cols = slice(j * P, (j + 1) * P)
            quantise(gated[:, j * P * PACK : (j + 1) * P * PACK], gated_codes[:, cols], gated_scales[:, cols])

        out_rows = out.flatten_outer_dims().rearrange("(p j) d -> p j d", j=TOKEN_TILES)

        def out_pass(j, first, end):
            acc = psum.tile([P, end - first], F32, tag="bank")
            nc.tensor.matmul_mx(
                out=acc[:],
                lhsT=gated_codes[:, j * P : (j + 1) * P].bitcast(FP8X4),
                lhsT_scale=gated_scales[:, j * P : (j + 1) * P],
                rhs=o[2][:, first:end].bitcast(FP8X4),
                rhs_scale=o[3][:, first:end],
                start=True,
                stop=True,
            )
            return acc

        def finish(j, first, end, acc, queue):
            result = keep.tile([P, end - first], F32, name="result%d_%d" % (j, first))
            nc.vector.tensor_tensor(out=result[:], in0=acc[:], in1=residual[:, j, first:end], op=mybir.AluOpType.add)
            queue.dma_start(out=out_rows[:, j, first:end], in_=result[:])

        keep_clock_up()
        keep_clock_up()
        keep_clock_up()
        out_b_bank = spread_out_b()
        add_residual(0, out_b_bank)
        add_residual(1, out_b_bank)
        bank_h = transpose(x[0][0][:])
        move_out(on_scalar, bank_h, x[0][1][:])
        quantise(x[0][1][:], x[0][2][:], x[0][3][:])
        bank_g = transpose(x[1][0][:])
        move_out(on_scalar, bank_g, x[1][1][:])
        quantise(x[1][1][:], x[1][2][:], x[1][3][:])
        keep_clock_up()
        bank_w0 = transpose(w[0][0][:])
        move_out(on_scalar, bank_w0, w[0][1][:])
        quantise(w[0][1][:], w[0][2][:], w[0][3][:])
        bank_w1 = transpose(w[1][0][:])
        move_out(on_scalar, bank_w1, w[1][1][:])
        quantise(w[1][1][:], w[1][2][:], w[1][3][:])
        go_b_bank = psum.tile([P, P], F32, tag="bank")
        nc.tensor.transpose(go_b_bank[:], go_b_rows[:].bitcast(F32), ident[:])
        go_b_cols = keep.tile([P, GATE_TILES], BF16)
        nc.scalar.copy(out=go_b_cols[:].bitcast(F32), in_=go_b_bank[:, 0:2])
        keep_clock_up()
        bank_w2 = transpose(w[2][0][:])
        move_out(on_scalar, bank_w2, w[2][1][:])
        bank_w3a = transpose(w[3][0][:, 0:512])
        bank_w3b = transpose(w[3][0][:, 512:1024])
        move_out(on_vector, bank_w3a, w[3][1][:, 0:512])
        move_out(on_scalar, bank_w3b, w[3][1][:, 512:1024])
        quantise(w[2][1][:], w[2][2][:], w[2][3][:])
        quantise(w[3][1][:], w[3][2][:], w[3][3][:])
        acc_0a = gate_passes(0, 0, TOKENS)
        sigmoid(0, 0, TOKENS, acc_0a)
        acc_10 = gate_passes(1, 0, P)
        sigmoid(1, 0, P, acc_10)
        bank_o0a = transpose(o[0][:, 0:512])
        bank_o0b = transpose(o[0][:, 512:1024])
        move_out(on_scalar, bank_o0b, o[1][:, 512:1024])
        acc_20 = gate_passes(2, 0, P)
        sigmoid(2, 0, P, acc_20)
        acc_30 = gate_passes(3, 0, P)
        sigmoid(3, 0, P, acc_30)
        move_out(on_vector, bank_o0a, o[1][:, 0:512])
        quantise(o[1][:, 0:1024], o[2][:, 0:256], o[3][:, 0:256])
        acc_11 = gate_passes(1, P, TOKENS)
        sigmoid(1, P, TOKENS, acc_11)
        acc_21 = gate_passes(2, P, TOKENS)
        sigmoid(2, P, TOKENS, acc_21)
        acc_31 = gate_passes(3, P, TOKENS)
        sigmoid(3, P, TOKENS, acc_31)
        product(0, 128)
        product(128, 192)
        quantise_gated(0)
        product(192, 256)
        bank_o1 = transpose(o[0][:, 1024:2048])
        keep_clock_up_mx(2)
        move_out(on_scalar, bank_o1, o[1][:, 1024:2048])
        quantise(o[1][:, 1024:2048], o[2][:, 256:512], o[3][:, 256:512])
        quantise_gated(1)
        out_00 = out_pass(0, 0, D // 2)
        finish(0, 0, D // 2, out_00, nc.sync)
        out_01 = out_pass(0, D // 2, D)
        finish(0, D // 2, D, out_01, nc.sync)
        out_10 = out_pass(1, 0, D // 2)
        finish(1, 0, D // 2, out_10, nc.sync)
        out_11 = out_pass(1, D // 2, D)
        finish(1, D // 2, D, out_11, nc.sync)
